import numpy as np
import ml_dtypes


def mxq(x, axis, fmt="e4m3"):
    dtype, down = {"e4m3": (ml_dtypes.float8_e4m3fn, 7), "e5m2": (ml_dtypes.float8_e5m2, 14)}[fmt]
    v = np.moveaxis(np.asarray(x, np.float32).astype(ml_dtypes.bfloat16).astype(np.float64), axis, -1)
    blocks = v.reshape(v.shape[:-1] + (-1, 32))
    amax = np.abs(blocks).max(-1, keepdims=True)
    byte = np.maximum(np.where(amax > 0, np.frexp(amax)[1] - 1 + 127, 0) - down, 1)
    scale = np.exp2(byte - 127.0)
    codes = (blocks / scale).astype(np.float32).astype(dtype).astype(np.float64)
    return np.moveaxis((codes * scale).reshape(v.shape), -1, axis)


WIDE = False


def mx_kscale(k):
    if not WIDE:
        return np.ones(k)
    levels = np.array([10, -10, 5, -5, 0])
    a = np.random.permutation(np.resize(levels, k // 512 * 4)).reshape(k // 512, 4)
    idx = np.arange(k)
    return np.exp2(a[idx // 512, idx % 128 // 32])


BF16 = ml_dtypes.bfloat16


def bf(x):
    return np.asarray(x, np.float32).astype(BF16)


def f64(x):
    return np.asarray(x).astype(np.float64)


B, N, W, D = 2, 2048, 512, 128
NW = N // W
NEG = -1.0e30


def setup_inputs():
    s = np.array(mx_kscale(N), dtype=np.float64)
    s[np.arange(N) % W < D] = s.max()
    a = np.log2(s)
    q = np.random.standard_normal((B, N, D)) / np.sqrt(D)
    ko = np.random.standard_normal((B, N, D))
    kp = np.random.standard_normal((B, N - W, D))
    q[:, :, 0] = np.log(2.0)
    ko[:, :, 0] += a
    kp[:, :, 0] += a[:N - W]
    v = np.random.standard_normal((B, N, D)) * 3.0 * (s.max() / s)[:, None]
    return {"q_rot": bf(q), "k_own": bf(ko), "k_prev": bf(kp), "v": bf(v)}


def reference(q_rot, k_own, k_prev, v):
    q = f64(q_rot).reshape(B, NW, W, D)
    ko = f64(k_own).reshape(B, NW, W, D)
    kp = f64(k_prev).reshape(B, NW - 1, W, D)
    vq = mxq(f64(v), 1, "e4m3")
    pos = np.arange(W)
    later = pos[:, None] < pos[None, :]
    s_own = np.where(later, NEG, q @ ko.transpose(0, 1, 3, 2))
    s_prev = q[:, 1:] @ kp.transpose(0, 1, 3, 2)
    s0 = s_own[:, 0]
    e0 = np.exp(s0 - s0.max(-1, keepdims=True))
    outs = [(mxq(e0, 2, "e4m3") @ vq[:, :W]) / e0.sum(-1, keepdims=True)]
    s = np.concatenate([s_prev, s_own[:, 1:]], axis=-1)
    e = np.exp(s - s.max(-1, keepdims=True))
    eq = mxq(e, 3, "e4m3")
    for t in range(1, NW):
        outs.append((eq[:, t - 1] @ vq[:, (t - 1) * W:(t + 1) * W]) / e[:, t - 1].sum(-1, keepdims=True))
    return np.concatenate(outs, axis=1)

@@ -1,0 +1,225 @@
+from contextlib import ExitStack
+
+import concourse.mybir as mybir
+from concourse.masks import make_identity
+
+BF16 = mybir.dt.bfloat16
+F32 = mybir.dt.float32
+U32 = mybir.dt.uint32
+U8 = mybir.dt.uint8
+FP8X4 = mybir.dt.float8_e4m3fn_x4
+ALU = mybir.AluOpType
+AX = mybir.AxisListType
+EXP = mybir.ActivationFunctionType.Exp
+
+B, N, W, D = 2, 2048, 512, 128
+P = 128
+PACK = 4
+NW = N // W
+WINDOWS = B * NW
+QT = W // P
+TILES = WINDOWS * QT
+DIAG = P // PACK
+NEG = -1.0e30
+PREV, OWN = 0, 1
+
+FLOPS = 2 * 2 * D * B * (W * W + (NW - 1) * W * 2 * W)
+
+
+def tile_localattention_pa_kernel(tc, q_rot, k_own, k_prev, v, out):
+    nc = tc.nc
+    with ExitStack() as ctx:
+        ctx.enter_context(tc.manual_schedule())
+        const = ctx.enter_context(tc.tile_pool(name="const", bufs=1))
+        loaded = ctx.enter_context(tc.tile_pool(name="loaded", bufs=1))
+        turned = ctx.enter_context(tc.tile_pool(name="turned", bufs=2))
+        work = ctx.enter_context(tc.tile_pool(name="work", bufs=2))
+        small = ctx.enter_context(tc.tile_pool(name="small", bufs=4))
+        psum = ctx.enter_context(tc.psum_pool(name="psum", bufs=2))
+
+        q_in, k_in, v_in = {}, {}, {}
+        for g in range(WINDOWS):
+            b, w = divmod(g, NW)
+            rows = slice(w * W, (w + 1) * W)
+            q_in[g] = loaded.tile([P, QT, D], BF16, name="q_in%d" % g)
+            nc.sync.dma_start(out=q_in[g][:], in_=q_rot[b, rows, :].rearrange("(a r) d -> r a d", r=P))
+            k_in[g, OWN] = loaded.tile([P, PACK, D], BF16, name="k_own_in%d" % g)
+            nc.sync.dma_start(out=k_in[g, OWN][:], in_=k_own[b, rows, :].rearrange("(p t) d -> p t d", t=PACK))
+            if w > 0:
+                before = slice((w - 1) * W, w * W)
+                k_in[g, PREV] = loaded.tile([P, PACK, D], BF16, name="k_prev_in%d" % g)
+                nc.sync.dma_start(
+                    out=k_in[g, PREV][:], in_=k_prev[b, before, :].rearrange("(p t) d -> p t d", t=PACK)
+                )
+            v_in[g] = loaded.tile([P, PACK, D], BF16, name="v_in%d" % g)
+            nc.sync.dma_start(out=v_in[g][:], in_=v[b, rows, :].rearrange("(p t) d -> p t d", t=PACK))
+
+        warm = const.tile([P, 1], F32, name="warm")
+        nc.vector.memset(warm[:], 0.0)
+        nc.scalar.activation(out=warm[:], in_=warm[:], func=EXP)
+        ident = const.tile([P, P], BF16, name="ident")
+        make_identity(nc, ident[:])
+        later_f32 = const.tile([P, PACK, DIAG], F32, name="later_f32")
+        nc.gpsimd.memset(later_f32[:], 0.0)
+        nc.gpsimd.affine_select(
+            out=later_f32[:],
+            in_=later_f32[:],
+            pattern=[[-1, PACK], [-PACK, DIAG]],
+            compare_op=ALU.is_ge,
+            fill=NEG,
+            base=0,
+            channel_multiplier=1,
+        )
+        later = const.tile([P, PACK, DIAG], BF16, name="later")
+        nc.vector.tensor_copy(out=later[:], in_=later_f32[:])
+        e_rows = []
+        for a in range(QT):
+            e_rows.append(const.tile([P, 2, PACK, P], BF16, name="e_rows%d" % a))
+            nc.gpsimd.memset(e_rows[a][:, OWN], 0.0)
+        v_codes = const.tile([P, WINDOWS, D], U32, name="v_codes", align_bytes=64)
+        v_scales = const.tile([P, WINDOWS, D], U8, name="v_scales", align_bytes=64)
+
+        qT, kT, v_grouped = {}, {}, {}
+        scores, neg_max, row_sums = {}, {}, {}
+        e_grouped, e_codes, e_scales, product = {}, {}, {}, {}
+
+        def units(g):
+            return [OWN] if g % NW == 0 else [PREV, OWN]
+
+        def seen(u, a):
+            return P if u == PREV else DIAG * (a + 1)
+
+        def turn(rows_in, tag):
+            bank = psum.tile([P, PACK, P], BF16, name="bank_" + tag, tag="flipped", bufs=3)
+            for j in range(PACK):
+                nc.tensor.transpose(bank[:, j, :], rows_in[:, j, :], ident[:])
+            cols = turned.tile([P, PACK, P], BF16, name=tag, tag=tag)
+            nc.vector.tensor_copy(out=cols[:], in_=bank[:])
+            return cols
+
+        def prepare(g, part):
+            if part == 0:
+                qT[g] = turn(q_in[g], "qT")
+            elif part == 1:
+                kT[g, OWN] = turn(k_in[g, OWN], "kT_own")
+            elif part == 2:
+                if PREV in units(g):
+                    kT[g, PREV] = turn(k_in[g, PREV], "kT_prev")
+                v_grouped[g] = work.tile([P, D, PACK], BF16, name="v_grouped", tag="v_grouped", align_bytes=64)
+                nc.vector.tensor_copy(out=v_grouped[g][:], in_=v_in[g][:].rearrange("p t d -> p d t"))
+            else:
+                nc.vector.quantize_mx(
+                    out=v_codes[:, g, :].bitcast(FP8X4),
+                    scales=v_scales[:, g, :],
+                    in_=v_grouped[g][:].rearrange("p d t -> p (d t)"),
+                )
+
+        def score(i):
+            g, a = divmod(i, QT)
+            row_max = small.tile([P, 2], F32, name="row_max", tag="row_max")
+            for u in units(g):
+                n = seen(u, a)
+                s = psum.tile([P, PACK, P], F32, name="scores%d" % u, tag="scores%d" % u)
+                nc.tensor.matmul(
+                    out=s[:, :, 0:n], lhsT=qT[g][:, a, :], rhs=kT[g, u][:, :, 0:n], start=True, stop=(u == PREV)
+                )
+                if u == OWN:
+                    nc.tensor.matmul(
+                        out=s[:, :, n - DIAG : n], lhsT=ident[:], rhs=later[:], start=False, stop=True
+                    )
+                nc.vector.reduce_max(out=row_max[:, u : u + 1], in_=s[:, :, 0:n], axis=AX.XY)
+                scores[i, u] = s
+            first = units(g)[0]
+            neg_max[i] = small.tile([P, 1], F32, name="neg_max", tag="neg_max")
+            nc.vector.tensor_scalar(
+                out=neg_max[i][:],
+                in0=row_max[:, first : first + 1],
+                scalar1=row_max[:, OWN : OWN + 1],
+                scalar2=-1.0,
+                op0=ALU.max,
+                op1=ALU.mult,
+            )
+
+        def exponential(i):
+            g, a = divmod(i, QT)
+            if a == 0:
+                row_sums[g] = small.tile([P, QT, 2], F32, name="row_sums", tag="row_sums")
+            for u in units(g):
+                n = seen(u, a)
+                nc.scalar.activation(
+                    out=e_rows[a][:, u, :, 0:n],
+                    in_=scores[i, u][:, :, 0:n],
+                    func=EXP,
+                    bias=neg_max[i][:],
+                    scale=1.0,
+                    accum_out=row_sums[g][:, a, u : u + 1],
+                )
+
+        def flip(i):
+            g, a = divmod(i, QT)
+            first = units(g)[0]
+            bank = psum.tile([P, 2, PACK, P], BF16, name="bank_e", tag="flipped", bufs=3)
+            for u in units(g):
+                for t in range(PACK):
+                    nc.tensor.transpose(bank[:, u, t, :], e_rows[a][:, u, t, :], ident[:])
+            e_grouped[i] = work.tile([P, 2, P, PACK], BF16, name="e_grouped", tag="e_grouped", align_bytes=64)
+            nc.scalar.copy(out=e_grouped[i][:, first:2], in_=bank[:, first:2].rearrange("p u t r -> p u r t"))
+
+        def quantise(i):
+            g, a = divmod(i, QT)
+            first = units(g)[0]
+            e_codes[i] = work.tile([P, 2, P], U32, name="e_codes", tag="e_codes", align_bytes=64)
+            e_scales[i] = work.tile([P, 2, P], U8, name="e_scales", tag="e_scales", align_bytes=64)
+            nc.vector.quantize_mx(
+                out=e_codes[i][:, first:2].rearrange("p u r -> p (u r)").bitcast(FP8X4),
+                scales=e_scales[i][:, first:2].rearrange("p u r -> p (u r)"),
+                in_=e_grouped[i][:, first:2].rearrange("p u r t -> p (u r t)"),
+            )
+
+        def multiply(i):
+            g, a = divmod(i, QT)
+            if a == 0:
+                product[g] = psum.tile([P, QT, D], F32, name="product", tag="product", bufs=1)
+            for u in units(g):
+                nc.tensor.matmul_mx(
+                    out=product[g][:, a, :],
+                    lhsT=e_codes[i][:, u, :].bitcast(FP8X4),
+                    lhsT_scale=e_scales[i][:, u, :],
+                    rhs=v_codes[:, g - 1 + u, :].bitcast(FP8X4),
+                    rhs_scale=v_scales[:, g - 1 + u, :],
+                    start=(u == units(g)[0]),
+                    stop=(u == OWN),
+                )
+            if a == QT - 1:
+                first = units(g)[0]
+                inverse = small.tile([P, QT], F32, name="inverse", tag="inverse")
+                nc.vector.reduce_sum(out=inverse[:], in_=row_sums[g][:, :, first:2], axis=AX.X)
+                nc.vector.reciprocal(out=inverse[:], in_=inverse[:])
+                result = work.tile([P, QT, D], F32, name="result", tag="result")
+                nc.vector.tensor_tensor(
+                    out=result[:],
+                    in0=product[g][:],
+                    in1=inverse[:].unsqueeze(2).to_broadcast([P, QT, D]),
+                    op=ALU.mult,
+                )
+                b, w = divmod(g, NW)
+                nc.sync.dma_start(
+                    out=out[b, w * W : (w + 1) * W, :].rearrange("(a r) d -> r a d", r=P), in_=result[:]
+                )
+
+        for part in range(QT):
+            prepare(0, part)
+        for step in range(TILES + 3):
+            if 0 <= step - 3:
+                quantise(step - 3)
+            if step < TILES:
+                score(step)
+            if 0 <= step - 1 < TILES:
+                exponential(step - 1)
+            if 0 <= step - 2 < TILES:
+                flip(step - 2)
+            if 0 <= step - 3:
+                multiply(step - 3)
+            g, a = divmod(step, QT)
+            if g + 1 < WINDOWS:
+                prepare(g + 1, a)

@@ -33,7 +33,7 @@ def tile_localattention_pa_kernel(tc, q_rot, k_own, k_prev, v, out):
         const = ctx.enter_context(tc.tile_pool(name="const", bufs=1))
         loaded = ctx.enter_context(tc.tile_pool(name="loaded", bufs=1))
         turned = ctx.enter_context(tc.tile_pool(name="turned", bufs=2))
-        work = ctx.enter_context(tc.tile_pool(name="work", bufs=2))
+        work = ctx.enter_context(tc.tile_pool(name="work", bufs=3))
         small = ctx.enter_context(tc.tile_pool(name="small", bufs=4))
         psum = ctx.enter_context(tc.psum_pool(name="psum", bufs=2))
 
@@ -80,7 +80,7 @@ def tile_localattention_pa_kernel(tc, q_rot, k_own, k_prev, v, out):
         v_scales = const.tile([P, WINDOWS, D], U8, name="v_scales", align_bytes=64)
 
         qT, kT, v_grouped = {}, {}, {}
-        scores, neg_max, row_sums = {}, {}, {}
+        scores, row_max, neg_max, row_sums = {}, {}, {}, {}
         e_grouped, e_codes, e_scales, product = {}, {}, {}, {}
 
         def units(g):
@@ -116,10 +116,10 @@ def tile_localattention_pa_kernel(tc, q_rot, k_own, k_prev, v, out):
 
         def score(i):
             g, a = divmod(i, QT)
-            row_max = small.tile([P, 2], F32, name="row_max", tag="row_max")
+            row_max[i] = small.tile([P, 2], F32, name="row_max", tag="row_max")
             for u in units(g):
                 n = seen(u, a)
-                s = psum.tile([P, PACK, P], F32, name="scores%d" % u, tag="scores%d" % u)
+                s = psum.tile([P, PACK, P], F32, name="scores", tag="scores", bufs=4)
                 nc.tensor.matmul(
                     out=s[:, :, 0:n], lhsT=qT[g][:, a, :], rhs=kT[g, u][:, :, 0:n], start=True, stop=(u == PREV)
                 )
@@ -127,14 +127,16 @@ def tile_localattention_pa_kernel(tc, q_rot, k_own, k_prev, v, out):
                     nc.tensor.matmul(
                         out=s[:, :, n - DIAG : n], lhsT=ident[:], rhs=later[:], start=False, stop=True
                     )
-                nc.vector.reduce_max(out=row_max[:, u : u + 1], in_=s[:, :, 0:n], axis=AX.XY)
+                nc.vector.reduce_max(out=row_max[i][:, u : u + 1], in_=s[:, :, 0:n], axis=AX.XY)
                 scores[i, u] = s
-            first = units(g)[0]
+
+        def negate_max(i):
+            first = units(i // QT)[0]
             neg_max[i] = small.tile([P, 1], F32, name="neg_max", tag="neg_max")
             nc.vector.tensor_scalar(
                 out=neg_max[i][:],
-                in0=row_max[:, first : first + 1],
-                scalar1=row_max[:, OWN : OWN + 1],
+                in0=row_max[i][:, first : first + 1],
+                scalar1=row_max[i][:, OWN : OWN + 1],
                 scalar2=-1.0,
                 op0=ALU.max,
                 op1=ALU.mult,
@@ -209,17 +211,19 @@ def tile_localattention_pa_kernel(tc, q_rot, k_own, k_prev, v, out):
 
         for part in range(QT):
             prepare(0, part)
-        for step in range(TILES + 3):
-            if 0 <= step - 3:
-                quantise(step - 3)
+        for step in range(TILES + 4):
             if step < TILES:
                 score(step)
+            if 0 <= step - 3 < TILES:
+                quantise(step - 3)
+            if step < TILES:
+                negate_max(step)
             if 0 <= step - 1 < TILES:
                 exponential(step - 1)
             if 0 <= step - 2 < TILES:
                 flip(step - 2)
-            if 0 <= step - 3:
-                multiply(step - 3)
+            if 0 <= step - 4:
+                multiply(step - 4)
             g, a = divmod(step, QT)
             if g + 1 < WINDOWS:
                 prepare(g + 1, a)

@@ -59,6 +59,8 @@ def tile_localattention_pa_kernel(tc, q_rot, k_own, k_prev, v, out):
         nc.scalar.activation(out=warm[:], in_=warm[:], func=EXP)
         ident = const.tile([P, P], BF16, name="ident")
         make_identity(nc, ident[:])
+        ident_f32 = const.tile([P, P], F32, name="ident_f32")
+        make_identity(nc, ident_f32[:])
         later_f32 = const.tile([P, PACK, DIAG], F32, name="later_f32")
         nc.gpsimd.memset(later_f32[:], 0.0)
         nc.gpsimd.affine_select(
@@ -74,7 +76,7 @@ def tile_localattention_pa_kernel(tc, q_rot, k_own, k_prev, v, out):
         nc.vector.tensor_copy(out=later[:], in_=later_f32[:])
         e_rows = []
         for a in range(QT):
-            e_rows.append(const.tile([P, 2, PACK, P], BF16, name="e_rows%d" % a))
+            e_rows.append(const.tile([P, 2, PACK * P], BF16, name="e_rows%d" % a))
             nc.gpsimd.memset(e_rows[a][:, OWN], 0.0)
         v_codes = const.tile([P, WINDOWS, D], U32, name="v_codes", align_bytes=64)
         v_scales = const.tile([P, WINDOWS, D], U8, name="v_scales", align_bytes=64)
@@ -149,8 +151,8 @@ def tile_localattention_pa_kernel(tc, q_rot, k_own, k_prev, v, out):
             for u in units(g):
                 n = seen(u, a)
                 nc.scalar.activation(
-                    out=e_rows[a][:, u, :, 0:n],
-                    in_=scores[i, u][:, :, 0:n],
+                    out=e_rows[a][:, u, :].rearrange("q (h p e) -> q h p e", h=2, e=2)[:, :, 0:n, :],
+                    in_=scores[i, u][:].rearrange("q (h e) p -> q h p e", e=2)[:, :, 0:n, :],
                     func=EXP,
                     bias=neg_max[i][:],
                     scale=1.0,
@@ -160,12 +162,16 @@ def tile_localattention_pa_kernel(tc, q_rot, k_own, k_prev, v, out):
         def flip(i):
             g, a = divmod(i, QT)
             first = units(g)[0]
-            bank = psum.tile([P, 2, PACK, P], BF16, name="bank_e", tag="flipped", bufs=3)
+            bank = psum.tile([P, 2, 2, P], F32, name="bank_e", tag="flipped", bufs=3)
             for u in units(g):
-                for t in range(PACK):
-                    nc.tensor.transpose(bank[:, u, t, :], e_rows[a][:, u, t, :], ident[:])
-            e_grouped[i] = work.tile([P, 2, P, PACK], BF16, name="e_grouped", tag="e_grouped", align_bytes=64)
-            nc.scalar.copy(out=e_grouped[i][:, first:2], in_=bank[:, first:2].rearrange("p u t r -> p u r t"))
+                words = e_rows[a][:, u, :].bitcast(F32)
+                for h in range(2):
+                    nc.tensor.transpose(bank[:, u, h, :], words[:, h * P : (h + 1) * P], ident_f32[:])
+            e_grouped[i] = work.tile([P, 2, P * PACK], BF16, name="e_grouped", tag="e_grouped", align_bytes=64)
+            nc.scalar.copy(
+                out=e_grouped[i][:, first:2, :].bitcast(F32).rearrange("p u (r h) -> p u r h", h=2),
+                in_=bank[:, first:2].rearrange("p u h r -> p u r h"),
+            )
 
         def quantise(i):
             g, a = divmod(i, QT)
@@ -175,7 +181,7 @@ def tile_localattention_pa_kernel(tc, q_rot, k_own, k_prev, v, out):
             nc.vector.quantize_mx(
                 out=e_codes[i][:, first:2].rearrange("p u r -> p (u r)").bitcast(FP8X4),
                 scales=e_scales[i][:, first:2].rearrange("p u r -> p (u r)"),
-                in_=e_grouped[i][:, first:2].rearrange("p u r t -> p (u r t)"),
+                in_=e_grouped[i][:, first:2, :].rearrange("p u c -> p (u c)"),
             )
 
         def multiply(i):

@@ -84,6 +84,7 @@ def tile_localattention_pa_kernel(tc, q_rot, k_own, k_prev, v, out):
         qT, kT, v_grouped = {}, {}, {}
         scores, row_max, neg_max, row_sums = {}, {}, {}, {}
         e_grouped, e_codes, e_scales, product = {}, {}, {}, {}
+        total, inverse = {}, {}
 
         def units(g):
             return [OWN] if g % NW == 0 else [PREV, OWN]
@@ -135,7 +136,7 @@ def tile_localattention_pa_kernel(tc, q_rot, k_own, k_prev, v, out):
         def negate_max(i):
             first = units(i // QT)[0]
             neg_max[i] = small.tile([P, 1], F32, name="neg_max", tag="neg_max")
-            nc.vector.tensor_scalar(
+            nc.gpsimd.tensor_scalar(
                 out=neg_max[i][:],
                 in0=row_max[i][:, first : first + 1],
                 scalar1=row_max[i][:, OWN : OWN + 1],
@@ -184,6 +185,17 @@ def tile_localattention_pa_kernel(tc, q_rot, k_own, k_prev, v, out):
                 in_=e_grouped[i][:, first:2, :].rearrange("p u c -> p (u c)"),
             )
 
+        def add_sums(g):
+            if PREV in units(g):
+                total[g] = small.tile([P, QT], F32, name="total", tag="total")
+                nc.gpsimd.tensor_tensor(
+                    out=total[g][:], in0=row_sums[g][:, :, PREV], in1=row_sums[g][:, :, OWN], op=ALU.add
+                )
+
+        def invert(g):
+            inverse[g] = small.tile([P, QT], F32, name="inverse", tag="inverse")
+            nc.vector.reciprocal(out=inverse[g][:], in_=total[g][:] if PREV in units(g) else row_sums[g][:, :, OWN])
+
         def multiply(i):
             g, a = divmod(i, QT)
             if a == 0:
@@ -199,15 +211,11 @@ def tile_localattention_pa_kernel(tc, q_rot, k_own, k_prev, v, out):
                     stop=(u == OWN),
                 )
             if a == QT - 1:
-                first = units(g)[0]
-                inverse = small.tile([P, QT], F32, name="inverse", tag="inverse")
-                nc.vector.reduce_sum(out=inverse[:], in_=row_sums[g][:, :, first:2], axis=AX.X)
-                nc.vector.reciprocal(out=inverse[:], in_=inverse[:])
                 result = work.tile([P, QT, D], F32, name="result", tag="result")
                 nc.vector.tensor_tensor(
                     out=result[:],
                     in0=product[g][:],
-                    in1=inverse[:].unsqueeze(2).to_broadcast([P, QT, D]),
+                    in1=inverse[g][:].unsqueeze(2).to_broadcast([P, QT, D]),
                     op=ALU.mult,
                 )
                 b, w = divmod(g, NW)
@@ -224,6 +232,10 @@ def tile_localattention_pa_kernel(tc, q_rot, k_own, k_prev, v, out):
                 quantise(step - 3)
             if step < TILES:
                 negate_max(step)
+            if step >= 2 and (step - 2) % QT == QT - 1:
+                add_sums((step - 2) // QT)
+            if step >= 3 and (step - 3) % QT == QT - 1:
+                invert((step - 3) // QT)
             if 0 <= step - 1 < TILES:
                 exponential(step - 1)
             if 0 <= step - 2 < TILES:

@@ -109,7 +109,14 @@ def tile_localattention_pa_kernel(tc, q_rot, k_own, k_prev, v, out):
                 if PREV in units(g):
                     kT[g, PREV] = turn(k_in[g, PREV], "kT_prev")
                 v_grouped[g] = work.tile([P, D, PACK], BF16, name="v_grouped", tag="v_grouped", align_bytes=64)
-                nc.vector.tensor_copy(out=v_grouped[g][:], in_=v_in[g][:].rearrange("p t d -> p d t"))
+                nc.gpsimd.tensor_scalar(
+                    out=v_grouped[g][:],
+                    in0=v_in[g][:].rearrange("p t d -> p d t"),
+                    scalar1=1.0,
+                    scalar2=0.0,
+                    op0=ALU.mult,
+                    op1=ALU.add,
+                )
             else:
                 nc.vector.quantize_mx(
                     out=v_codes[:, g, :].bitcast(FP8X4),

@@ -28,6 +28,23 @@ FLOPS = 2 * 2 * D * B * (W * W + (NW - 1) * W * 2 * W)
 
 def tile_localattention_pa_kernel(tc, q_rot, k_own, k_prev, v, out):
     nc = tc.nc
+    order = [0, 1, 2, 3, 5, 6, 7, 4]
+    last = order[-1]
+    tiles = []
+    for g in order:
+        tiles.extend((g, a) for a in ([2, 3, 1, 0] if g == last else range(QT)))
+
+    def units(g):
+        return [OWN] if g % NW == 0 else [PREV, OWN]
+
+    def seen(u, a):
+        return P if u == PREV else DIAG * (a + 1)
+
+    values, have = [], []
+    for g in order:
+        values.append([x for x in (g - 1 + u for u in units(g)) if x not in have])
+        have.extend(values[-1])
+
     with ExitStack() as ctx:
         ctx.enter_context(tc.manual_schedule())
         const = ctx.enter_context(tc.tile_pool(name="const", bufs=1))
@@ -38,7 +55,7 @@ def tile_localattention_pa_kernel(tc, q_rot, k_own, k_prev, v, out):
         psum = ctx.enter_context(tc.psum_pool(name="psum", bufs=2))
 
         q_in, k_in, v_in = {}, {}, {}
-        for g in range(WINDOWS):
+        for k, g in enumerate(order):
             b, w = divmod(g, NW)
             rows = slice(w * W, (w + 1) * W)
             q_in[g] = loaded.tile([P, QT, D], BF16, name="q_in%d" % g)
@@ -51,8 +68,12 @@ def tile_localattention_pa_kernel(tc, q_rot, k_own, k_prev, v, out):
                 nc.sync.dma_start(
                     out=k_in[g, PREV][:], in_=k_prev[b, before, :].rearrange("(p t) d -> p t d", t=PACK)
                 )
-            v_in[g] = loaded.tile([P, PACK, D], BF16, name="v_in%d" % g)
-            nc.sync.dma_start(out=v_in[g][:], in_=v[b, rows, :].rearrange("(p t) d -> p t d", t=PACK))
+            for x in values[k]:
+                bx, wx = divmod(x, NW)
+                v_in[x] = loaded.tile([P, PACK, D], BF16, name="v_in%d" % x)
+                nc.sync.dma_start(
+                    out=v_in[x][:], in_=v[bx, wx * W : (wx + 1) * W, :].rearrange("(p t) d -> p t d", t=PACK)
+                )
 
         warm = const.tile([P, 1], F32, name="warm")
         nc.vector.memset(warm[:], 0.0)
@@ -77,7 +98,7 @@ def tile_localattention_pa_kernel(tc, q_rot, k_own, k_prev, v, out):
         e_rows = []
         for a in range(QT):
             e_rows.append(const.tile([P, 2, PACK * P], BF16, name="e_rows%d" % a))
-            nc.gpsimd.memset(e_rows[a][:, OWN], 0.0)
+            nc.vector.memset(e_rows[a][:, OWN], 0.0)
         v_codes = const.tile([P, WINDOWS, D], U32, name="v_codes", align_bytes=64)
         v_scales = const.tile([P, WINDOWS, D], U8, name="v_scales", align_bytes=64)
 
@@ -86,46 +107,34 @@ def tile_localattention_pa_kernel(tc, q_rot, k_own, k_prev, v, out):
         e_grouped, e_codes, e_scales, product = {}, {}, {}, {}
         total, inverse = {}, {}
 
-        def units(g):
-            return [OWN] if g % NW == 0 else [PREV, OWN]
-
-        def seen(u, a):
-            return P if u == PREV else DIAG * (a + 1)
-
-        def turn(rows_in, tag):
+        def turn(rows_in, tag, copy):
             bank = psum.tile([P, PACK, P], BF16, name="bank_" + tag, tag="flipped", bufs=3)
             for j in range(PACK):
                 nc.tensor.transpose(bank[:, j, :], rows_in[:, j, :], ident[:])
             cols = turned.tile([P, PACK, P], BF16, name=tag, tag=tag)
-            nc.vector.tensor_copy(out=cols[:], in_=bank[:])
+            copy(out=cols[:], in_=bank[:])
             return cols
 
-        def prepare(g, part):
-            if part == 0:
-                qT[g] = turn(q_in[g], "qT")
-            elif part == 1:
-                kT[g, OWN] = turn(k_in[g, OWN], "kT_own")
-            elif part == 2:
-                if PREV in units(g):
-                    kT[g, PREV] = turn(k_in[g, PREV], "kT_prev")
-                v_grouped[g] = work.tile([P, D, PACK], BF16, name="v_grouped", tag="v_grouped", align_bytes=64)
-                nc.gpsimd.tensor_scalar(
-                    out=v_grouped[g][:],
-                    in0=v_in[g][:].rearrange("p t d -> p d t"),
-                    scalar1=1.0,
-                    scalar2=0.0,
-                    op0=ALU.mult,
-                    op1=ALU.add,
-                )
-            else:
-                nc.vector.quantize_mx(
-                    out=v_codes[:, g, :].bitcast(FP8X4),
-                    scales=v_scales[:, g, :],
-                    in_=v_grouped[g][:].rearrange("p d t -> p (d t)"),
-                )
+        def group_values(x):
+            v_grouped[x] = work.tile([P, D, PACK], BF16, name="v_grouped", tag="v_grouped", align_bytes=64)
+            nc.gpsimd.tensor_scalar(
+                out=v_grouped[x][:],
+                in0=v_in[x][:].rearrange("p t d -> p d t"),
+                scalar1=1.0,
+                scalar2=0.0,
+                op0=ALU.mult,
+                op1=ALU.add,
+            )
+
+        def quantise_values(x):
+            nc.vector.quantize_mx(
+                out=v_codes[:, x, :].bitcast(FP8X4),
+                scales=v_scales[:, x, :],
+                in_=v_grouped[x][:].rearrange("p d t -> p (d t)"),
+            )
 
         def score(i):
-            g, a = divmod(i, QT)
+            g, a = tiles[i]
             row_max[i] = small.tile([P, 2], F32, name="row_max", tag="row_max")
             for u in units(g):
                 n = seen(u, a)
@@ -141,7 +150,7 @@ def tile_localattention_pa_kernel(tc, q_rot, k_own, k_prev, v, out):
                 scores[i, u] = s
 
         def negate_max(i):
-            first = units(i // QT)[0]
+            first = units(tiles[i][0])[0]
             neg_max[i] = small.tile([P, 1], F32, name="neg_max", tag="neg_max")
             nc.gpsimd.tensor_scalar(
                 out=neg_max[i][:],
@@ -153,8 +162,8 @@ def tile_localattention_pa_kernel(tc, q_rot, k_own, k_prev, v, out):
             )
 
         def exponential(i):
-            g, a = divmod(i, QT)
-            if a == 0:
+            g, a = tiles[i]
+            if i % QT == 0:
                 row_sums[g] = small.tile([P, QT, 2], F32, name="row_sums", tag="row_sums")
             for u in units(g):
                 n = seen(u, a)
@@ -168,7 +177,7 @@ def tile_localattention_pa_kernel(tc, q_rot, k_own, k_prev, v, out):
                 )
 
         def flip(i):
-            g, a = divmod(i, QT)
+            g, a = tiles[i]
             first = units(g)[0]
             bank = psum.tile([P, 2, 2, P], F32, name="bank_e", tag="flipped", bufs=3)
             for u in units(g):
@@ -182,8 +191,7 @@ def tile_localattention_pa_kernel(tc, q_rot, k_own, k_prev, v, out):
             )
 
         def quantise(i):
-            g, a = divmod(i, QT)
-            first = units(g)[0]
+            first = units(tiles[i][0])[0]
             e_codes[i] = work.tile([P, 2, P], U32, name="e_codes", tag="e_codes", align_bytes=64)
             e_scales[i] = work.tile([P, 2, P], U8, name="e_scales", tag="e_scales", align_bytes=64)
             nc.vector.quantize_mx(
@@ -203,13 +211,16 @@ def tile_localattention_pa_kernel(tc, q_rot, k_own, k_prev, v, out):
             inverse[g] = small.tile([P, QT], F32, name="inverse", tag="inverse")
             nc.vector.reciprocal(out=inverse[g][:], in_=total[g][:] if PREV in units(g) else row_sums[g][:, :, OWN])
 
-        def multiply(i):
-            g, a = divmod(i, QT)
-            if a == 0:
-                product[g] = psum.tile([P, QT, D], F32, name="product", tag="product", bufs=1)
+        def invert_tile(i):
+            g, a = tiles[i]
+            inverse[i] = small.tile([P, 1], F32, name="inverse_tile", tag="inverse_tile")
+            nc.vector.reciprocal(out=inverse[i][:], in_=row_sums[g][:, a, OWN : OWN + 1])
+
+        def passes(i, acc):
+            g, a = tiles[i]
             for u in units(g):
                 nc.tensor.matmul_mx(
-                    out=product[g][:, a, :],
+                    out=acc,
                     lhsT=e_codes[i][:, u, :].bitcast(FP8X4),
                     lhsT_scale=e_scales[i][:, u, :],
                     rhs=v_codes[:, g - 1 + u, :].bitcast(FP8X4),
@@ -217,7 +228,23 @@ def tile_localattention_pa_kernel(tc, q_rot, k_own, k_prev, v, out):
                     start=(u == units(g)[0]),
                     stop=(u == OWN),
                 )
-            if a == QT - 1:
+
+        def multiply(i):
+            g, a = tiles[i]
+            b, w = divmod(g, NW)
+            if g == last:
+                alone = psum.tile([P, D], F32, name="alone", tag="flipped", bufs=3)
+                passes(i, alone[:])
+                part = work.tile([P, D], F32, name="part", tag="part")
+                nc.vector.tensor_scalar(
+                    out=part[:], in0=alone[:], scalar1=inverse[i][:], scalar2=None, op0=ALU.mult
+                )
+                nc.sync.dma_start(out=out[b, w * W + a * P : w * W + (a + 1) * P, :], in_=part[:])
+                return
+            if i % QT == 0:
+                product[g] = psum.tile([P, QT, D], F32, name="product", tag="product", bufs=1)
+            passes(i, product[g][:, a, :])
+            if i % QT == QT - 1:
                 result = work.tile([P, QT, D], F32, name="result", tag="result")
                 nc.vector.tensor_tensor(
                     out=result[:],
@@ -225,30 +252,43 @@ def tile_localattention_pa_kernel(tc, q_rot, k_own, k_prev, v, out):
                     in1=inverse[g][:].unsqueeze(2).to_broadcast([P, QT, D]),
                     op=ALU.mult,
                 )
-                b, w = divmod(g, NW)
                 nc.sync.dma_start(
                     out=out[b, w * W : (w + 1) * W, :].rearrange("(a r) d -> r a d", r=P), in_=result[:]
                 )
 
-        for part in range(QT):
-            prepare(0, part)
+        qT[order[0]] = turn(q_in[order[0]], "qT", nc.scalar.copy)
+        kT[order[0], OWN] = turn(k_in[order[0], OWN], "kT_own", nc.vector.tensor_copy)
         for step in range(TILES + 4):
+            k, part = divmod(step, QT)
             if step < TILES:
                 score(step)
             if 0 <= step - 3 < TILES:
                 quantise(step - 3)
             if step < TILES:
                 negate_max(step)
-            if step >= 2 and (step - 2) % QT == QT - 1:
-                add_sums((step - 2) // QT)
-            if step >= 3 and (step - 3) % QT == QT - 1:
-                invert((step - 3) // QT)
+            if step >= 2 and (step - 2) % QT == QT - 1 and order[(step - 2) // QT] != last:
+                add_sums(order[(step - 2) // QT])
+            if step >= 3 and (step - 3) % QT == QT - 1 and order[(step - 3) // QT] != last:
+                invert(order[(step - 3) // QT])
+            if 0 <= step - 2 < TILES and tiles[step - 2][0] == last:
+                invert_tile(step - 2)
             if 0 <= step - 1 < TILES:
                 exponential(step - 1)
             if 0 <= step - 2 < TILES:
                 flip(step - 2)
             if 0 <= step - 4:
                 multiply(step - 4)
-            g, a = divmod(step, QT)
-            if g + 1 < WINDOWS:
-                prepare(g + 1, a)
+            if k < WINDOWS:
+                for j, x in enumerate(values[k]):
+                    if part == j + 2:
+                        quantise_values(x)
+                    if part == j + 1:
+                        group_values(x)
+            if k + 1 < WINDOWS:
+                g = order[k + 1]
+                if part == 0:
+                    qT[g] = turn(q_in[g], "qT", nc.vector.tensor_copy)
+                elif part == 1:
+                    kT[g, OWN] = turn(k_in[g, OWN], "kT_own", nc.vector.tensor_copy)
+                elif part == 2 and PREV in units(g):
+                    kT[g, PREV] = turn(k_in[g, PREV], "kT_prev", nc.vector.tensor_copy)

@@ -80,6 +80,11 @@ def tile_localattention_pa_kernel(tc, q_rot, k_own, k_prev, v, out):
         nc.scalar.activation(out=warm[:], in_=warm[:], func=EXP)
         ident = const.tile([P, P], BF16, name="ident")
         make_identity(nc, ident[:])
+        zeros = const.tile([P, PACK, P], BF16, name="zeros")
+        nc.vector.memset(zeros[:], 0.0)
+        for n in range(4):
+            unread = psum.tile([P, PACK, P], F32, name="unread", tag="scores", bufs=4)
+            nc.tensor.matmul(out=unread[:], lhsT=ident[:], rhs=zeros[:], start=True, stop=True)
         ident_f32 = const.tile([P, P], F32, name="ident_f32")
         make_identity(nc, ident_f32[:])
         later_f32 = const.tile([P, PACK, DIAG], F32, name="later_f32")
@@ -146,15 +151,20 @@ def tile_localattention_pa_kernel(tc, q_rot, k_own, k_prev, v, out):
                     nc.tensor.matmul(
                         out=s[:, :, n - DIAG : n], lhsT=ident[:], rhs=later[:], start=False, stop=True
                     )
-                nc.vector.reduce_max(out=row_max[i][:, u : u + 1], in_=s[:, :, 0:n], axis=AX.XY)
+                nc.vector.reduce_max(
+                    out=row_max[i][:, u : u + 1], in_=s[:, :, 0:n], axis=AX.XY, negate=(PREV not in units(g))
+                )
                 scores[i, u] = s
 
         def negate_max(i):
-            first = units(tiles[i][0])[0]
-            neg_max[i] = small.tile([P, 1], F32, name="neg_max", tag="neg_max")
+            if PREV not in units(tiles[i][0]):
+                neg_max[i] = row_max[i][:, OWN : OWN + 1]
+                return
+            both = small.tile([P, 1], F32, name="neg_max", tag="neg_max")
+            neg_max[i] = both[:]
             nc.gpsimd.tensor_scalar(
-                out=neg_max[i][:],
-                in0=row_max[i][:, first : first + 1],
+                out=both[:],
+                in0=row_max[i][:, PREV : PREV + 1],
                 scalar1=row_max[i][:, OWN : OWN + 1],
                 scalar2=-1.0,
                 op0=ALU.max,
@@ -171,7 +181,7 @@ def tile_localattention_pa_kernel(tc, q_rot, k_own, k_prev, v, out):
                     out=e_rows[a][:, u, :].rearrange("q (h p e) -> q h p e", h=2, e=2)[:, :, 0:n, :],
                     in_=scores[i, u][:].rearrange("q (h e) p -> q h p e", e=2)[:, :, 0:n, :],
                     func=EXP,
-                    bias=neg_max[i][:],
+                    bias=neg_max[i],
                     scale=1.0,
                     accum_out=row_sums[g][:, a, u : u + 1],
                 )

@@ -296,9 +296,10 @@ def tile_localattention_pa_kernel(tc, q_rot, k_own, k_prev, v, out):
                         group_values(x)
             if k + 1 < WINDOWS:
                 g = order[k + 1]
+                copy = nc.vector.tensor_copy if PREV in units(order[k]) else nc.scalar.copy
                 if part == 0:
-                    qT[g] = turn(q_in[g], "qT", nc.vector.tensor_copy)
+                    qT[g] = turn(q_in[g], "qT", copy)
                 elif part == 1:
-                    kT[g, OWN] = turn(k_in[g, OWN], "kT_own", nc.vector.tensor_copy)
+                    kT[g, OWN] = turn(k_in[g, OWN], "kT_own", copy)
                 elif part == 2 and PREV in units(g):
-                    kT[g, PREV] = turn(k_in[g, PREV], "kT_prev", nc.vector.tensor_copy)
+                    kT[g, PREV] = turn(k_in[g, PREV], "kT_prev", copy)

@@ -288,11 +288,19 @@ def tile_localattention_pa_kernel(tc, q_rot, k_own, k_prev, v, out):
                 flip(step - 2)
             if 0 <= step - 4:
                 multiply(step - 4)
-            if k < WINDOWS:
+            if k == 0:
                 for j, x in enumerate(values[k]):
                     if part == j + 2:
                         quantise_values(x)
                     if part == j + 1:
+                        group_values(x)
+            if 1 <= k < WINDOWS:
+                for j, x in enumerate(values[k]):
+                    if part == j:
+                        quantise_values(x)
+            if k + 1 < WINDOWS:
+                for j, x in enumerate(values[k + 1]):
+                    if part == QT - len(values[k + 1]) + j:
                         group_values(x)
             if k + 1 < WINDOWS:
                 g = order[k + 1]

from contextlib import ExitStack

import concourse.mybir as mybir
from concourse.masks import make_identity

BF16 = mybir.dt.bfloat16
F32 = mybir.dt.float32
U32 = mybir.dt.uint32
U8 = mybir.dt.uint8
FP8X4 = mybir.dt.float8_e4m3fn_x4
ALU = mybir.AluOpType
AX = mybir.AxisListType
EXP = mybir.ActivationFunctionType.Exp

B, N, W, D = 2, 2048, 512, 128
P = 128
PACK = 4
NW = N // W
WINDOWS = B * NW
QT = W // P
TILES = WINDOWS * QT
DIAG = P // PACK
NEG = -1.0e30
PREV, OWN = 0, 1

FLOPS = 2 * 2 * D * B * (W * W + (NW - 1) * W * 2 * W)


def tile_localattention_pa_kernel(tc, q_rot, k_own, k_prev, v, out):
    nc = tc.nc
    order = [0, 1, 2, 3, 5, 6, 7, 4]
    last = order[-1]
    tiles = []
    for g in order:
        tiles.extend((g, a) for a in ([2, 3, 1, 0] if g == last else range(QT)))

    def units(g):
        return [OWN] if g % NW == 0 else [PREV, OWN]

    def seen(u, a):
        return P if u == PREV else DIAG * (a + 1)

    values, have = [], []
    for g in order:
        values.append([x for x in (g - 1 + u for u in units(g)) if x not in have])
        have.extend(values[-1])

    with ExitStack() as ctx:
        ctx.enter_context(tc.manual_schedule())
        const = ctx.enter_context(tc.tile_pool(name="const", bufs=1))
        loaded = ctx.enter_context(tc.tile_pool(name="loaded", bufs=1))
        turned = ctx.enter_context(tc.tile_pool(name="turned", bufs=2))
        work = ctx.enter_context(tc.tile_pool(name="work", bufs=3))
        small = ctx.enter_context(tc.tile_pool(name="small", bufs=4))
        psum = ctx.enter_context(tc.psum_pool(name="psum", bufs=2))

        q_in, k_in, v_in = {}, {}, {}
        for k, g in enumerate(order):
            b, w = divmod(g, NW)
            rows = slice(w * W, (w + 1) * W)
            q_in[g] = loaded.tile([P, QT, D], BF16, name="q_in%d" % g)
            nc.sync.dma_start(out=q_in[g][:], in_=q_rot[b, rows, :].rearrange("(a r) d -> r a d", r=P))
            k_in[g, OWN] = loaded.tile([P, PACK, D], BF16, name="k_own_in%d" % g)
            nc.sync.dma_start(out=k_in[g, OWN][:], in_=k_own[b, rows, :].rearrange("(p t) d -> p t d", t=PACK))
            if w > 0:
                before = slice((w - 1) * W, w * W)
                k_in[g, PREV] = loaded.tile([P, PACK, D], BF16, name="k_prev_in%d" % g)
                nc.sync.dma_start(
                    out=k_in[g, PREV][:], in_=k_prev[b, before, :].rearrange("(p t) d -> p t d", t=PACK)
                )
            for x in values[k]:
                bx, wx = divmod(x, NW)
                v_in[x] = loaded.tile([P, PACK, D], BF16, name="v_in%d" % x)
                nc.sync.dma_start(
                    out=v_in[x][:], in_=v[bx, wx * W : (wx + 1) * W, :].rearrange("(p t) d -> p t d", t=PACK)
                )

        warm = const.tile([P, 1], F32, name="warm")
        nc.vector.memset(warm[:], 0.0)
        nc.scalar.activation(out=warm[:], in_=warm[:], func=EXP)
        ident = const.tile([P, P], BF16, name="ident")
        make_identity(nc, ident[:])
        zeros = const.tile([P, PACK, P], BF16, name="zeros")
        nc.vector.memset(zeros[:], 0.0)
        for n in range(4):
            unread = psum.tile([P, PACK, P], F32, name="unread", tag="scores", bufs=4)
            nc.tensor.matmul(out=unread[:], lhsT=ident[:], rhs=zeros[:], start=True, stop=True)
        ident_f32 = const.tile([P, P], F32, name="ident_f32")
        make_identity(nc, ident_f32[:])
        later_f32 = const.tile([P, PACK, DIAG], F32, name="later_f32")
        nc.gpsimd.memset(later_f32[:], 0.0)
        nc.gpsimd.affine_select(
            out=later_f32[:],
            in_=later_f32[:],
            pattern=[[-1, PACK], [-PACK, DIAG]],
            compare_op=ALU.is_ge,
            fill=NEG,
            base=0,
            channel_multiplier=1,
        )
        later = const.tile([P, PACK, DIAG], BF16, name="later")
        nc.vector.tensor_copy(out=later[:], in_=later_f32[:])
        e_rows = []
        for a in range(QT):
            e_rows.append(const.tile([P, 2, PACK * P], BF16, name="e_rows%d" % a))
            nc.vector.memset(e_rows[a][:, OWN], 0.0)
        v_codes = const.tile([P, WINDOWS, D], U32, name="v_codes", align_bytes=64)
        v_scales = const.tile([P, WINDOWS, D], U8, name="v_scales", align_bytes=64)

        qT, kT, v_grouped = {}, {}, {}
        scores, row_max, neg_max, row_sums = {}, {}, {}, {}
        e_grouped, e_codes, e_scales, product = {}, {}, {}, {}
        total, inverse = {}, {}

        def turn(rows_in, tag, copy):
            bank = psum.tile([P, PACK, P], BF16, name="bank_" + tag, tag="flipped", bufs=3)
            for j in range(PACK):
                nc.tensor.transpose(bank[:, j, :], rows_in[:, j, :], ident[:])
            cols = turned.tile([P, PACK, P], BF16, name=tag, tag=tag)
            copy(out=cols[:], in_=bank[:])
            return cols

        def group_values(x):
            v_grouped[x] = work.tile([P, D, PACK], BF16, name="v_grouped", tag="v_grouped", align_bytes=64)
            nc.gpsimd.tensor_scalar(
                out=v_grouped[x][:],
                in0=v_in[x][:].rearrange("p t d -> p d t"),
                scalar1=1.0,
                scalar2=0.0,
                op0=ALU.mult,
                op1=ALU.add,
            )

        def quantise_values(x):
            nc.vector.quantize_mx(
                out=v_codes[:, x, :].bitcast(FP8X4),
                scales=v_scales[:, x, :],
                in_=v_grouped[x][:].rearrange("p d t -> p (d t)"),
            )

        def score(i):
            g, a = tiles[i]
            row_max[i] = small.tile([P, 2], F32, name="row_max", tag="row_max")
            for u in units(g):
                n = seen(u, a)
                s = psum.tile([P, PACK, P], F32, name="scores", tag="scores", bufs=4)
                nc.tensor.matmul(
                    out=s[:, :, 0:n], lhsT=qT[g][:, a, :], rhs=kT[g, u][:, :, 0:n], start=True, stop=(u == PREV)
                )
                if u == OWN:
                    nc.tensor.matmul(
                        out=s[:, :, n - DIAG : n], lhsT=ident[:], rhs=later[:], start=False, stop=True
                    )
                nc.vector.reduce_max(
                    out=row_max[i][:, u : u + 1], in_=s[:, :, 0:n], axis=AX.XY, negate=(PREV not in units(g))
                )
                scores[i, u] = s

        def negate_max(i):
            if PREV not in units(tiles[i][0]):
                neg_max[i] = row_max[i][:, OWN : OWN + 1]
                return
            both = small.tile([P, 1], F32, name="neg_max", tag="neg_max")
            neg_max[i] = both[:]
            nc.gpsimd.tensor_scalar(
                out=both[:],
                in0=row_max[i][:, PREV : PREV + 1],
                scalar1=row_max[i][:, OWN : OWN + 1],
                scalar2=-1.0,
                op0=ALU.max,
                op1=ALU.mult,
            )

        def exponential(i):
            g, a = tiles[i]
            if i % QT == 0:
                row_sums[g] = small.tile([P, QT, 2], F32, name="row_sums", tag="row_sums")
            for u in units(g):
                n = seen(u, a)
                nc.scalar.activation(
                    out=e_rows[a][:, u, :].rearrange("q (h p e) -> q h p e", h=2, e=2)[:, :, 0:n, :],
                    in_=scores[i, u][:].rearrange("q (h e) p -> q h p e", e=2)[:, :, 0:n, :],
                    func=EXP,
                    bias=neg_max[i],
                    scale=1.0,
                    accum_out=row_sums[g][:, a, u : u + 1],
                )

        def flip(i):
            g, a = tiles[i]
            first = units(g)[0]
            bank = psum.tile([P, 2, 2, P], F32, name="bank_e", tag="flipped", bufs=3)
            for u in units(g):
                words = e_rows[a][:, u, :].bitcast(F32)
                for h in range(2):
                    nc.tensor.transpose(bank[:, u, h, :], words[:, h * P : (h + 1) * P], ident_f32[:])
            e_grouped[i] = work.tile([P, 2, P * PACK], BF16, name="e_grouped", tag="e_grouped", align_bytes=64)
            nc.scalar.copy(
                out=e_grouped[i][:, first:2, :].bitcast(F32).rearrange("p u (r h) -> p u r h", h=2),
                in_=bank[:, first:2].rearrange("p u h r -> p u r h"),
            )

        def quantise(i):
            first = units(tiles[i][0])[0]
            e_codes[i] = work.tile([P, 2, P], U32, name="e_codes", tag="e_codes", align_bytes=64)
            e_scales[i] = work.tile([P, 2, P], U8, name="e_scales", tag="e_scales", align_bytes=64)
            nc.vector.quantize_mx(
                out=e_codes[i][:, first:2].rearrange("p u r -> p (u r)").bitcast(FP8X4),
                scales=e_scales[i][:, first:2].rearrange("p u r -> p (u r)"),
                in_=e_grouped[i][:, first:2, :].rearrange("p u c -> p (u c)"),
            )

        def add_sums(g):
            if PREV in units(g):
                total[g] = small.tile([P, QT], F32, name="total", tag="total")
                nc.gpsimd.tensor_tensor(
                    out=total[g][:], in0=row_sums[g][:, :, PREV], in1=row_sums[g][:, :, OWN], op=ALU.add
                )

        def invert(g):
            inverse[g] = small.tile([P, QT], F32, name="inverse", tag="inverse")
            nc.vector.reciprocal(out=inverse[g][:], in_=total[g][:] if PREV in units(g) else row_sums[g][:, :, OWN])

        def invert_tile(i):
            g, a = tiles[i]
            inverse[i] = small.tile([P, 1], F32, name="inverse_tile", tag="inverse_tile")
            nc.vector.reciprocal(out=inverse[i][:], in_=row_sums[g][:, a, OWN : OWN + 1])

        def passes(i, acc):
            g, a = tiles[i]
            for u in units(g):
                nc.tensor.matmul_mx(
                    out=acc,
                    lhsT=e_codes[i][:, u, :].bitcast(FP8X4),
                    lhsT_scale=e_scales[i][:, u, :],
                    rhs=v_codes[:, g - 1 + u, :].bitcast(FP8X4),
                    rhs_scale=v_scales[:, g - 1 + u, :],
                    start=(u == units(g)[0]),
                    stop=(u == OWN),
                )

        def multiply(i):
            g, a = tiles[i]
            b, w = divmod(g, NW)
            if g == last:
                alone = psum.tile([P, D], F32, name="alone", tag="flipped", bufs=3)
                passes(i, alone[:])
                part = work.tile([P, D], F32, name="part", tag="part")
                nc.vector.tensor_scalar(
                    out=part[:], in0=alone[:], scalar1=inverse[i][:], scalar2=None, op0=ALU.mult
                )
                nc.sync.dma_start(out=out[b, w * W + a * P : w * W + (a + 1) * P, :], in_=part[:])
                return
            if i % QT == 0:
                product[g] = psum.tile([P, QT, D], F32, name="product", tag="product", bufs=1)
            passes(i, product[g][:, a, :])
            if i % QT == QT - 1:
                result = work.tile([P, QT, D], F32, name="result", tag="result")
                nc.vector.tensor_tensor(
                    out=result[:],
                    in0=product[g][:],
                    in1=inverse[g][:].unsqueeze(2).to_broadcast([P, QT, D]),
                    op=ALU.mult,
                )
                nc.sync.dma_start(
                    out=out[b, w * W : (w + 1) * W, :].rearrange("(a r) d -> r a d", r=P), in_=result[:]
                )

        qT[order[0]] = turn(q_in[order[0]], "qT", nc.scalar.copy)
        kT[order[0], OWN] = turn(k_in[order[0], OWN], "kT_own", nc.vector.tensor_copy)
        for step in range(TILES + 4):
            k, part = divmod(step, QT)
            if step < TILES:
                score(step)
            if 0 <= step - 3 < TILES:
                quantise(step - 3)
            if step < TILES:
                negate_max(step)
            if step >= 2 and (step - 2) % QT == QT - 1 and order[(step - 2) // QT] != last:
                add_sums(order[(step - 2) // QT])
            if step >= 3 and (step - 3) % QT == QT - 1 and order[(step - 3) // QT] != last:
                invert(order[(step - 3) // QT])
            if 0 <= step - 2 < TILES and tiles[step - 2][0] == last:
                invert_tile(step - 2)
            if 0 <= step - 1 < TILES:
                exponential(step - 1)
            if 0 <= step - 2 < TILES:
                flip(step - 2)
            if 0 <= step - 4:
                multiply(step - 4)
            if k == 0:
                for j, x in enumerate(values[k]):
                    if part == j + 2:
                        quantise_values(x)
                    if part == j + 1:
                        group_values(x)
            if 1 <= k < WINDOWS:
                for j, x in enumerate(values[k]):
                    if part == j:
                        quantise_values(x)
            if k + 1 < WINDOWS:
                for j, x in enumerate(values[k + 1]):
                    if part == QT - len(values[k + 1]) + j:
                        group_values(x)
            if k + 1 < WINDOWS:
                g = order[k + 1]
                copy = nc.vector.tensor_copy if PREV in units(order[k]) else nc.scalar.copy
                if part == 0:
                    qT[g] = turn(q_in[g], "qT", copy)
                elif part == 1:
                    kT[g, OWN] = turn(k_in[g, OWN], "kT_own", copy)
                elif part == 2 and PREV in units(g):
                    kT[g, PREV] = turn(k_in[g, PREV], "kT_prev", copy)
